import numpy as np
import ml_dtypes


def mxq(x, axis, fmt="e4m3"):
    dtype, down = {"e4m3": (ml_dtypes.float8_e4m3fn, 7), "e5m2": (ml_dtypes.float8_e5m2, 14)}[fmt]
    v = np.moveaxis(np.asarray(x, np.float32).astype(ml_dtypes.bfloat16).astype(np.float64), axis, -1)
    blocks = v.reshape(v.shape[:-1] + (-1, 32))
    amax = np.abs(blocks).max(-1, keepdims=True)
    byte = np.maximum(np.where(amax > 0, np.frexp(amax)[1] - 1 + 127, 0) - down, 1)
    scale = np.exp2(byte - 127.0)
    codes = (blocks / scale).astype(np.float32).astype(dtype).astype(np.float64)
    return np.moveaxis((codes * scale).reshape(v.shape), -1, axis)


WIDE = False


def mx_kscale(k):
    if not WIDE:
        return np.ones(k)
    levels = np.array([10, -10, 5, -5, 0])
    a = np.random.permutation(np.resize(levels, k // 512 * 4)).reshape(k // 512, 4)
    idx = np.arange(k)
    return np.exp2(a[idx // 512, idx % 128 // 32])


BF16 = ml_dtypes.bfloat16


def bf(x):
    return np.asarray(x, np.float32).astype(BF16)


def f64(x):
    return np.asarray(x).astype(np.float64)


E2M1 = np.array([0.0, 0.5, 1.0, 1.5, 2.0, 3.0, 4.0, 6.0, -0.0, -0.5, -1.0, -1.5, -2.0, -3.0, -4.0, -6.0])


def pack_weight(w, fmt):
    k, n = w.shape
    w = f64(bf(w)).reshape(k // 32, 32, n)
    amax = np.abs(w).max(1)
    if fmt == "e4m3":
        byte = np.frexp(amax)[1] - 1 + 127 - 7
    else:
        mant, ex = np.frexp(amax / 6.0)
        byte = np.where(mant > 0.5, ex, ex - 1) + 127
    byte = np.clip(np.where(amax > 0, byte, 1), 1, 254)
    scaled = (w * np.exp2(127.0 - byte)[:, None, :]).reshape(k, n).astype(np.float32)
    by_word = np.ascontiguousarray(scaled.reshape(k // 512, 128, 4, n).transpose(0, 1, 3, 2))
    if fmt == "e4m3":
        words = by_word.astype(ml_dtypes.float8_e4m3fn).view(np.uint8)
    else:
        c = by_word.astype(ml_dtypes.float4_e2m1fn).view(np.uint8) & 0xF
        words = c[..., 0::2] | (c[..., 1::2] << 4)
    return np.ascontiguousarray(words), np.ascontiguousarray(byte.astype(np.uint8).reshape(k // 512, 16, n))


def unpack_weight(words, scales, fmt):
    g, p, n, _ = words.shape
    if fmt == "e4m3":
        vals = np.ascontiguousarray(words).view(ml_dtypes.float8_e4m3fn).astype(np.float64)
    else:
        nib = np.empty((g, p, n, 4), np.uint8)
        nib[..., 0::2] = words & 0xF
        nib[..., 1::2] = words >> 4
        vals = E2M1[nib]
    vals = vals * np.repeat(np.exp2(scales.astype(np.float64) - 127.0), 8, axis=1)[..., None]
    return vals.transpose(0, 1, 3, 2).reshape(g * 512, n)


B, N, H, DH, E, W, DQ, DKV = 1, 512, 4, 128, 2, 256, 1024, 8192
DV = E * DH
DM = H * DV
NEG = -3.4028234663852886e38


def silu(v):
    return v / (1.0 + np.exp(-v))


def split_heads(t):
    return t.reshape(B, N, H, DV).transpose(0, 2, 1, 3)


def setup_inputs():
    s = mx_kscale(DKV)
    q = bf(np.random.standard_normal((B, H, N, DH)) * 1.4)
    k1 = bf(np.random.standard_normal((B, H, N, DH)) * 1.4)
    key_values_input = bf(np.random.standard_normal((B, N, DKV)) * s)
    words, scales = pack_weight(np.random.standard_normal((DKV, DM)) * 4.0 / np.sqrt(DKV) / s[:, None], "e4m3")
    attn_sink = bf(np.log(N) + 0.5 + 0.5 * np.random.standard_normal(H))
    return {"q": q,
            "k1": k1,
            "key_values_input": key_values_input,
            "Wv1_words": words,
            "Wv1_scales": scales,
            "attn_sink": attn_sink}


def reference(q, k1, key_values_input, Wv1_words, Wv1_scales, attn_sink):
    v1 = split_heads(mxq(f64(key_values_input), 2, "e4m3") @ unpack_weight(Wv1_words, Wv1_scales, "e4m3"))
    sim = f64(q) @ f64(k1).transpose(0, 1, 3, 2) * DH ** -0.5
    idx = np.arange(N)
    mask = (idx[None, :] > idx[:, None]) & (idx[None, :] - idx[:, None] <= W)
    sim = np.where(mask, NEG, sim)
    sink = f64(attn_sink)[None, :, None, None]
    m = np.maximum(sim.max(-1, keepdims=True), sink)
    e = np.exp(sim - m)
    den = e.sum(-1, keepdims=True) + np.exp(sink - m)
    return silu((mxq(e, 3, "e4m3") @ mxq(v1, 2, "e4m3")) / den)

@@ -1,0 +1,374 @@
+from contextlib import ExitStack
+
+import concourse.masks as masks
+import concourse.mybir as mybir
+
+BF16 = mybir.dt.bfloat16
+F32 = mybir.dt.float32
+I32 = mybir.dt.int32
+U32 = mybir.dt.uint32
+U8 = mybir.dt.uint8
+FP8X4 = mybir.dt.float8_e4m3fn_x4
+ALU = mybir.AluOpType
+FUNC = mybir.ActivationFunctionType
+AXIS = mybir.AxisListType
+
+P = 128
+PACK = 4
+K_PASS = P * PACK
+N = 512
+H = 4
+DH = 128
+DV = 256
+DKV = 8192
+DM = H * DV
+WINDOW = 256
+GROUPS = DKV // K_PASS
+STEP_GROUPS = 2
+STEPS = GROUPS // STEP_GROUPS
+CHUNK = STEP_GROUPS * K_PASS
+EARLY = 2 * DV
+TILES = H * PACK
+PLANES = 4
+SCALE = DH ** -0.5
+BIG = 3.4028234663852886e38
+
+FLOPS = 2 * N * DKV * DM + H * (2 * N * N * DH + 2 * N * N * DV)
+
+
+def tile_attention_pa_k_kernel(tc, q, k1, key_values_input, Wv1_words, Wv1_scales, attn_sink, out):
+    nc = tc.nc
+    with ExitStack() as ctx:
+        ctx.enter_context(tc.manual_schedule())
+        keep = ctx.enter_context(tc.tile_pool(name="keep", bufs=1))
+        stream = ctx.enter_context(tc.tile_pool(name="stream", bufs=3))
+        pair = ctx.enter_context(tc.tile_pool(name="pair", bufs=2))
+        psum = ctx.enter_context(tc.psum_pool(name="psum", bufs=4))
+
+        x_rows = key_values_input[0].rearrange("(x y) k -> x y k", y=PACK)
+        w_words = Wv1_words.rearrange("g r n t -> g r (n t)").bitcast(I32).rearrange("g r n -> r g n")
+
+        k_rows = keep.tile([P, H, PACK, DH], BF16)
+        q_rows = keep.tile([P, H, PACK, DH], BF16)
+        for heads in (slice(0, 2), slice(2, H)):
+            nc.sync.dma_start(out=q_rows[:, heads], in_=q[0, heads].rearrange("h (x y) d -> x h y d", y=PACK))
+            nc.sync.dma_start(out=k_rows[:, heads], in_=k1[0, heads].rearrange("h (x y) d -> x h y d", y=PACK))
+        sink_bf = keep.tile([P, H], BF16)
+        nc.scalar.dma_start(out=sink_bf[:], in_=attn_sink.partition_broadcast(P))
+
+        w_planes = keep.tile([P, GROUPS // PLANES, DM], U8, align_bytes=64)
+        nc.vector.memset(w_planes[:].bitcast(I32), 0)
+        for a in range(GROUPS // PLANES):
+            for quadrant in range(4):
+                nc.sync.dma_start(
+                    out=w_planes[32 * quadrant : 32 * quadrant + 4 * PLANES, a, :].bitcast(I32),
+                    in_=Wv1_scales[PLANES * a : PLANES * (a + 1), 4 * quadrant : 4 * quadrant + 4, :].bitcast(I32),
+                )
+
+        def w_plane(g, columns):
+            return w_planes[4 * (g % PLANES) : P, g // PLANES, columns]
+
+        band = keep.tile([P, 2 * PACK - 1, P], F32)
+        nc.vector.memset(band[:], BIG)
+        ident_bf = keep.tile([P, P], BF16)
+        masks.make_identity(nc, ident_bf[:])
+        for base, fill in ((PACK - 1, -BIG), (WINDOW + PACK - 1, BIG)):
+            nc.gpsimd.affine_select(
+                out=band[:],
+                in_=band[:],
+                pattern=[[-1, 2 * PACK - 1], [-PACK, P]],
+                compare_op=ALU.is_ge,
+                fill=fill,
+                base=base,
+                channel_multiplier=PACK,
+            )
+        ident_f32 = keep.tile([P, P], F32)
+        masks.make_identity(nc, ident_f32[:])
+
+        def band_of(u):
+            return band[:, PACK - 1 - u : 2 * PACK - 1 - u, :].rearrange("x a z -> x (a z)")
+
+        warm = keep.tile([P, 1], F32)
+        nc.vector.memset(warm[:], 0.0)
+        nc.scalar.activation(out=warm[:], in_=warm[:], func=FUNC.Exp)
+
+        sink = keep.tile([P, H], F32)
+        nc.vector.tensor_copy(out=sink[:], in_=sink_bf[:])
+        neg_sink = keep.tile([P, H], F32)
+        nc.vector.tensor_scalar_mul(out=neg_sink[:], in0=sink_bf[:], scalar1=-1.0)
+
+        x_chunks = {}
+        w_chunks = {}
+
+        def load_step(s):
+            x_chunk = stream.tile([P, PACK, CHUNK], BF16)
+            nc.sync.dma_start(out=x_chunk[:], in_=x_rows[:, :, CHUNK * s : CHUNK * (s + 1)])
+            x_chunks[s] = x_chunk
+            w_chunk = stream.tile([P, STEP_GROUPS, EARLY], I32, align_bytes=64)
+            nc.sync.dma_start(out=w_chunk[:], in_=w_words[:, STEP_GROUPS * s : STEP_GROUPS * (s + 1), 0:EARLY])
+            w_chunks[s] = w_chunk
+
+        for s in range(3):
+            load_step(s)
+
+        q_t = keep.tile([P, H, PACK, P], BF16)
+        k_t = keep.tile([P, H, PACK, P], BF16)
+        for h in range(H):
+            q_bank = psum.tile([P, PACK, P], BF16, tag="acc")
+            k_bank = psum.tile([P, PACK, P], BF16, tag="work")
+            for y in range(PACK):
+                nc.tensor.transpose(q_bank[:, y, :], q_rows[:, h, y, :], ident_bf[:])
+            for y in range(PACK):
+                nc.tensor.transpose(k_bank[:, y, :], k_rows[:, h, y, :], ident_bf[:])
+            nc.vector.tensor_copy(out=q_t[:, h], in_=q_bank[:])
+            nc.scalar.copy(out=k_t[:, h], in_=k_bank[:])
+
+        scores = keep.tile([P, TILES, N], F32)
+
+        def score_bank(h, u, tag):
+            bank = psum.tile([P, N], F32, tag=tag)
+            nc.tensor.matmul(
+                bank[:], lhsT=q_t[:, h, u, :], rhs=k_t[:, h].rearrange("d y z -> d (y z)"), start=True, stop=True
+            )
+            return bank
+
+        for h in range(2):
+            for u in range(PACK):
+                bank = score_bank(h, u, "acc")
+                nc.vector.tensor_tensor(out=scores[:, PACK * h + u, :], in0=bank[:], in1=band_of(u), op=ALU.min)
+                bank = score_bank(h + 2, u, "work")
+                nc.scalar.copy(out=scores[:, PACK * (h + 2) + u, :], in_=bank[:])
+
+        def mask_in_sbuf(i):
+            nc.vector.tensor_tensor(out=scores[:, i, :], in0=scores[:, i, :], in1=band_of(i % PACK), op=ALU.min)
+
+        weights = keep.tile([P, TILES, N], BF16)
+        row_max = keep.tile([P, TILES], F32)
+        neg_max = keep.tile([P, TILES], F32)
+        row_sum = keep.tile([P, TILES], F32)
+        sink_term = keep.tile([P, TILES], F32)
+        denominator = keep.tile([P, TILES], F32)
+        inv_den = keep.tile([P, TILES], F32)
+
+        def row_maxima(j):
+            h = 2 * j // PACK
+            both = slice(2 * j, 2 * j + 2)
+            nc.vector.tensor_reduce(out=row_max[:, both], in_=scores[:, both, :], axis=AXIS.X, op=ALU.max)
+            nc.vector.tensor_scalar(
+                out=neg_max[:, both],
+                in0=row_max[:, both],
+                scalar1=-SCALE,
+                scalar2=neg_sink[:, h : h + 1],
+                op0=ALU.mult,
+                op1=ALU.min,
+            )
+
+        def exponentials(j):
+            for i in (2 * j, 2 * j + 1):
+                nc.scalar.activation(
+                    out=weights[:, i, :],
+                    in_=scores[:, i, :],
+                    func=FUNC.Exp,
+                    bias=neg_max[:, i : i + 1],
+                    scale=SCALE,
+                    accum_out=row_sum[:, i : i + 1],
+                )
+
+        def denominators():
+            for h in range(H):
+                of_head = slice(PACK * h, PACK * (h + 1))
+                nc.scalar.activation(
+                    out=sink_term[:, of_head], in_=neg_max[:, of_head], func=FUNC.Exp, bias=sink[:, h : h + 1]
+                )
+            nc.vector.tensor_tensor(out=denominator[:], in0=row_sum[:], in1=sink_term[:], op=ALU.add)
+            nc.vector.reciprocal(out=inv_den[:], in_=denominator[:])
+
+        x_codes = keep.tile([P, GROUPS, N], U32, align_bytes=64)
+        x_planes = keep.tile([P, GROUPS, N], U8, align_bytes=64)
+        x_grouped = {}
+
+        def transpose_x(s):
+            for local in range(STEP_GROUPS):
+                grouped = pair.tile([P, N * PACK], BF16, tag="x_grouped", align_bytes=64)
+                x_grouped[STEP_GROUPS * s + local] = grouped
+                for half in range(2):
+                    bank = psum.tile([P, 2, 2, P], F32, tag="work")
+                    for y in range(2):
+                        words = x_chunks[s][:, 2 * half + y, :].bitcast(F32)
+                        first = (K_PASS // 2) * local
+                        for w in range(2):
+                            nc.tensor.transpose(
+                                bank[:, w, y, :], words[:, first + w : first + K_PASS // 2 : 2], ident_f32[:]
+                            )
+                    target = grouped[:].bitcast(F32)[:, N * half : N * (half + 1)].rearrange("r (c w) -> r c w", w=2)
+                    source = bank[:].rearrange("r w y x -> r (y x) w")
+                    if local == STEP_GROUPS - 1 and half == 1:
+                        nc.vector.tensor_copy(out=target, in_=source)
+                    else:
+                        nc.scalar.copy(out=target, in_=source)
+
+        def quantise_x(s):
+            for g in range(STEP_GROUPS * s, STEP_GROUPS * (s + 1)):
+                nc.vector.quantize_mx(
+                    out=x_codes[:, g, :].bitcast(FP8X4), scales=x_planes[:, g, :], in_=x_grouped[g][:]
+                )
+
+        def project(bank, g, y, w_codes, columns):
+            tokens = slice(P * y, P * (y + 1))
+            nc.tensor.matmul_mx(
+                out=bank,
+                lhsT=x_codes[:, g, tokens].bitcast(FP8X4),
+                lhsT_scale=x_planes[:, g, tokens],
+                rhs=w_codes.bitcast(FP8X4),
+                rhs_scale=w_plane(g, columns),
+                start=(g == 0),
+                stop=(g == GROUPS - 1),
+            )
+
+        w_late = keep.tile([P, GROUPS, DM - EARLY], I32, align_bytes=64)
+
+        def load_late():
+            for a in range(4):
+                part = slice(4 * a, 4 * (a + 1))
+                nc.sync.dma_start(out=w_late[:, part, :], in_=w_words[:, part, EARLY:DM])
+
+        early_banks = []
+        for y in range(PACK):
+            early_banks.append(psum.tile([P, EARLY], F32, tag="acc", name="early%d" % y))
+
+        transpose_x(0)
+        quantise_x(0)
+        for s in range(STEPS):
+            mask_in_sbuf(TILES // 2 + s)
+            row_maxima(s)
+            if s + 1 < STEPS:
+                transpose_x(s + 1)
+            for local in range(STEP_GROUPS):
+                for y in range(PACK):
+                    project(early_banks[y][:], STEP_GROUPS * s + local, y, w_chunks[s][:, local, :], slice(0, EARLY))
+            if s + 3 < STEPS:
+                load_step(s + 3)
+            if s + 3 == STEPS:
+                load_late()
+            exponentials(s)
+            if s + 1 < STEPS:
+                quantise_x(s + 1)
+
+        v_codes = keep.tile([P, H, DV], U32, align_bytes=64)
+        v_planes = keep.tile([P, H, DV], U8, align_bytes=64)
+        v_rounded = {}
+        v_grouped = {}
+
+        def round_values(h, y, product):
+            if y == 0:
+                v_rounded[h] = pair.tile([P, PACK, DV], BF16, tag="v_rounded", name="v_rounded%d" % h)
+            if y % 2 == 0:
+                nc.scalar.copy(out=v_rounded[h][:, y, :], in_=product)
+            else:
+                nc.vector.tensor_copy(out=v_rounded[h][:, y, :], in_=product)
+
+        def regroup_values(h):
+            grouped = pair.tile([P, DV, PACK], BF16, tag="v_grouped", align_bytes=64)
+            v_grouped[h] = grouped
+            nc.vector.tensor_copy(out=grouped[:], in_=v_rounded[h][:].rearrange("x y c -> x c y"))
+
+        def quantise_values(h):
+            nc.vector.quantize_mx(
+                out=v_codes[:, h, :].bitcast(FP8X4),
+                scales=v_planes[:, h, :],
+                in_=v_grouped[h][:].rearrange("x c y -> x (c y)"),
+            )
+
+        e_codes = keep.tile([P, H, N], U32, align_bytes=64)
+        e_planes = keep.tile([P, H, N], U8, align_bytes=64)
+        e_grouped = {}
+
+        def transpose_weights(h):
+            grouped = pair.tile([P, PACK, P, PACK], BF16, tag="e_grouped", align_bytes=64)
+            e_grouped[h] = grouped
+            for half in range(2):
+                bank = psum.tile([P, 2, PACK, P], BF16, tag="work")
+                for u in range(2):
+                    for y in range(PACK):
+                        nc.tensor.transpose(
+                            bank[:, u, y, :], weights[:, PACK * h + 2 * half + u, P * y : P * (y + 1)], ident_bf[:]
+                        )
+                target = grouped[:, 2 * half : 2 * half + 2, :, :]
+                source = bank[:].rearrange("z u y x -> z u x y")
+                if half == 0:
+                    nc.scalar.copy(out=target, in_=source)
+                else:
+                    nc.vector.tensor_copy(out=target, in_=source)
+
+        def quantise_weights(h):
+            nc.vector.quantize_mx(
+                out=e_codes[:, h, :].bitcast(FP8X4),
+                scales=e_planes[:, h, :],
+                in_=e_grouped[h][:].rearrange("z u x y -> z (u x y)"),
+            )
+
+        def attend(h):
+            result = pair.tile([P, PACK, DV], F32, tag="result")
+            for half in range(2):
+                bank = psum.tile([P, 2, DV], F32, tag="work")
+                for local in range(2):
+                    queries = slice(P * (2 * half + local), P * (2 * half + local + 1))
+                    nc.tensor.matmul_mx(
+                        out=bank[:, local, :],
+                        lhsT=e_codes[:, h, queries].bitcast(FP8X4),
+                        lhsT_scale=e_planes[:, h, queries],
+                        rhs=v_codes[:, h, :].bitcast(FP8X4),
+                        rhs_scale=v_planes[:, h, :],
+                        start=True,
+                        stop=True,
+                    )
+                for local in range(2):
+                    u = 2 * half + local
+                    nc.scalar.activation(
+                        out=result[:, u, :],
+                        in_=bank[:, local, :],
+                        func=FUNC.Silu,
+                        scale=inv_den[:, PACK * h + u : PACK * h + u + 1],
+                    )
+                done = slice(2 * half, 2 * half + 2)
+                rows = out[0, h].rearrange("(x u) c -> x u c", u=PACK)
+                nc.sync.dma_start(out=rows[:, done, :], in_=result[:, done, :])
+
+        def project_late(h, y):
+            bank = psum.tile([P, DV], F32, tag="acc")
+            for g in range(GROUPS):
+                project(bank[:], g, y, w_late[:, g, DV * h - EARLY : DV * (h + 1) - EARLY], slice(DV * h, DV * (h + 1)))
+            round_values(h, y, bank[:])
+
+        for h in range(2):
+            for y in range(PACK):
+                round_values(h, y, early_banks[y][:, DV * h : DV * (h + 1)])
+        transpose_weights(0)
+        transpose_weights(1)
+        regroup_values(0)
+        regroup_values(1)
+        quantise_weights(0)
+        quantise_weights(1)
+        quantise_values(0)
+        quantise_values(1)
+        denominators()
+        project_late(2, 0)
+        project_late(2, 1)
+        attend(0)
+        attend(1)
+        project_late(2, 2)
+        project_late(2, 3)
+        transpose_weights(2)
+        transpose_weights(3)
+        regroup_values(2)
+        quantise_weights(2)
+        quantise_weights(3)
+        quantise_values(2)
+        project_late(3, 0)
+        project_late(3, 1)
+        attend(2)
+        project_late(3, 2)
+        project_late(3, 3)
+        regroup_values(3)
+        quantise_values(3)
+        attend(3)

@@ -27,6 +27,11 @@ GROUPS = DKV // K_PASS
 STEP_GROUPS = 2
 STEPS = GROUPS // STEP_GROUPS
 CHUNK = STEP_GROUPS * K_PASS
+LOADS_AHEAD = 3
+SORT_AHEAD = 2
+LAST_X_STEP = STEPS - 1 - LOADS_AHEAD - SORT_AHEAD
+LATE_GROUPS = 4
+assert SORT_AHEAD == H // 2
 EARLY = 2 * DV
 TILES = H * PACK
 PLANES = 4
@@ -41,8 +46,6 @@ def tile_attention_pa_k_kernel(tc, q, k1, key_values_input, Wv1_words, Wv1_scale
     with ExitStack() as ctx:
         ctx.enter_context(tc.manual_schedule())
         keep = ctx.enter_context(tc.tile_pool(name="keep", bufs=1))
-        stream = ctx.enter_context(tc.tile_pool(name="stream", bufs=3))
-        pair = ctx.enter_context(tc.tile_pool(name="pair", bufs=2))
         psum = ctx.enter_context(tc.psum_pool(name="psum", bufs=4))
 
         x_rows = key_values_input[0].rearrange("(x y) k -> x y k", y=PACK)
@@ -97,51 +100,7 @@ def tile_attention_pa_k_kernel(tc, q, k1, key_values_input, Wv1_words, Wv1_scale
         neg_sink = keep.tile([P, H], F32)
         nc.vector.tensor_scalar_mul(out=neg_sink[:], in0=sink_bf[:], scalar1=-1.0)
 
-        x_chunks = {}
-        w_chunks = {}
-
-        def load_step(s):
-            x_chunk = stream.tile([P, PACK, CHUNK], BF16)
-            nc.sync.dma_start(out=x_chunk[:], in_=x_rows[:, :, CHUNK * s : CHUNK * (s + 1)])
-            x_chunks[s] = x_chunk
-            w_chunk = stream.tile([P, STEP_GROUPS, EARLY], I32, align_bytes=64)
-            nc.sync.dma_start(out=w_chunk[:], in_=w_words[:, STEP_GROUPS * s : STEP_GROUPS * (s + 1), 0:EARLY])
-            w_chunks[s] = w_chunk
-
-        for s in range(3):
-            load_step(s)
-
-        q_t = keep.tile([P, H, PACK, P], BF16)
-        k_t = keep.tile([P, H, PACK, P], BF16)
-        for h in range(H):
-            q_bank = psum.tile([P, PACK, P], BF16, tag="acc")
-            k_bank = psum.tile([P, PACK, P], BF16, tag="work")
-            for y in range(PACK):
-                nc.tensor.transpose(q_bank[:, y, :], q_rows[:, h, y, :], ident_bf[:])
-            for y in range(PACK):
-                nc.tensor.transpose(k_bank[:, y, :], k_rows[:, h, y, :], ident_bf[:])
-            nc.vector.tensor_copy(out=q_t[:, h], in_=q_bank[:])
-            nc.scalar.copy(out=k_t[:, h], in_=k_bank[:])
-
         scores = keep.tile([P, TILES, N], F32)
-
-        def score_bank(h, u, tag):
-            bank = psum.tile([P, N], F32, tag=tag)
-            nc.tensor.matmul(
-                bank[:], lhsT=q_t[:, h, u, :], rhs=k_t[:, h].rearrange("d y z -> d (y z)"), start=True, stop=True
-            )
-            return bank
-
-        for h in range(2):
-            for u in range(PACK):
-                bank = score_bank(h, u, "acc")
-                nc.vector.tensor_tensor(out=scores[:, PACK * h + u, :], in0=bank[:], in1=band_of(u), op=ALU.min)
-                bank = score_bank(h + 2, u, "work")
-                nc.scalar.copy(out=scores[:, PACK * (h + 2) + u, :], in_=bank[:])
-
-        def mask_in_sbuf(i):
-            nc.vector.tensor_tensor(out=scores[:, i, :], in0=scores[:, i, :], in1=band_of(i % PACK), op=ALU.min)
-
         weights = keep.tile([P, TILES, N], BF16)
         row_max = keep.tile([P, TILES], F32)
         neg_max = keep.tile([P, TILES], F32)
@@ -150,21 +109,24 @@ def tile_attention_pa_k_kernel(tc, q, k1, key_values_input, Wv1_words, Wv1_scale
         denominator = keep.tile([P, TILES], F32)
         inv_den = keep.tile([P, TILES], F32)
 
-        def row_maxima(j):
-            h = 2 * j // PACK
-            both = slice(2 * j, 2 * j + 2)
-            nc.vector.tensor_reduce(out=row_max[:, both], in_=scores[:, both, :], axis=AXIS.X, op=ALU.max)
+        def mask_in_sbuf(i):
+            nc.vector.tensor_tensor(out=scores[:, i, :], in0=scores[:, i, :], in1=band_of(i % PACK), op=ALU.min)
+
+        def row_maxima(first, count):
+            h = first // PACK
+            these = slice(first, first + count)
+            nc.vector.tensor_reduce(out=row_max[:, these], in_=scores[:, these, :], axis=AXIS.X, op=ALU.max)
             nc.vector.tensor_scalar(
-                out=neg_max[:, both],
-                in0=row_max[:, both],
+                out=neg_max[:, these],
+                in0=row_max[:, these],
                 scalar1=-SCALE,
                 scalar2=neg_sink[:, h : h + 1],
                 op0=ALU.mult,
                 op1=ALU.min,
             )
 
-        def exponentials(j):
-            for i in (2 * j, 2 * j + 1):
+        def exponentials(first, count):
+            for i in range(first, first + count):
                 nc.scalar.activation(
                     out=weights[:, i, :],
                     in_=scores[:, i, :],
@@ -185,33 +147,13 @@ def tile_attention_pa_k_kernel(tc, q, k1, key_values_input, Wv1_words, Wv1_scale
 
         x_codes = keep.tile([P, GROUPS, N], U32, align_bytes=64)
         x_planes = keep.tile([P, GROUPS, N], U8, align_bytes=64)
-        x_grouped = {}
-
-        def transpose_x(s):
-            for local in range(STEP_GROUPS):
-                grouped = pair.tile([P, N * PACK], BF16, tag="x_grouped", align_bytes=64)
-                x_grouped[STEP_GROUPS * s + local] = grouped
-                for half in range(2):
-                    bank = psum.tile([P, 2, 2, P], F32, tag="work")
-                    for y in range(2):
-                        words = x_chunks[s][:, 2 * half + y, :].bitcast(F32)
-                        first = (K_PASS // 2) * local
-                        for w in range(2):
-                            nc.tensor.transpose(
-                                bank[:, w, y, :], words[:, first + w : first + K_PASS // 2 : 2], ident_f32[:]
-                            )
-                    target = grouped[:].bitcast(F32)[:, N * half : N * (half + 1)].rearrange("r (c w) -> r c w", w=2)
-                    source = bank[:].rearrange("r w y x -> r (y x) w")
-                    if local == STEP_GROUPS - 1 and half == 1:
-                        nc.vector.tensor_copy(out=target, in_=source)
-                    else:
-                        nc.scalar.copy(out=target, in_=source)
-
-        def quantise_x(s):
-            for g in range(STEP_GROUPS * s, STEP_GROUPS * (s + 1)):
-                nc.vector.quantize_mx(
-                    out=x_codes[:, g, :].bitcast(FP8X4), scales=x_planes[:, g, :], in_=x_grouped[g][:]
-                )
+        w_late = keep.tile([P, GROUPS, DM - EARLY], I32, align_bytes=64)
+        v_codes = keep.tile([P, H, DV], U32, align_bytes=64)
+        v_planes = keep.tile([P, H, DV], U8, align_bytes=64)
+        e_codes = keep.tile([P, H, N], U32, align_bytes=64)
+        e_planes = keep.tile([P, H, N], U8, align_bytes=64)
+        q_t = keep.tile([P, H, PACK, P], BF16)
+        k_t = keep.tile([P, H, PACK, P], BF16)
 
         def project(bank, g, y, w_codes, columns):
             tokens = slice(P * y, P * (y + 1))
@@ -225,150 +167,233 @@ def tile_attention_pa_k_kernel(tc, q, k1, key_values_input, Wv1_words, Wv1_scale
                 stop=(g == GROUPS - 1),
             )
 
-        w_late = keep.tile([P, GROUPS, DM - EARLY], I32, align_bytes=64)
+        early_banks = []
+        with tc.tile_pool(name="stream", bufs=LOADS_AHEAD) as stream, tc.tile_pool(name="turn", bufs=2) as turn:
+            x_chunks = {}
+            w_chunks = {}
+            x_sorted = {}
+            x_grouped = {}
 
-        def load_late():
-            for a in range(4):
-                part = slice(4 * a, 4 * (a + 1))
+            def load_x(s):
+                x_chunk = stream.tile([P, PACK, CHUNK], BF16)
+                nc.sync.dma_start(out=x_chunk[:], in_=x_rows[:, :, CHUNK * s : CHUNK * (s + 1)])
+                x_chunks[s] = x_chunk
+
+            def load_w(s):
+                w_chunk = stream.tile([P, STEP_GROUPS, EARLY], I32, align_bytes=64)
+                nc.sync.dma_start(out=w_chunk[:], in_=w_words[:, STEP_GROUPS * s : STEP_GROUPS * (s + 1), 0:EARLY])
+                w_chunks[s] = w_chunk
+
+            def load_late(a):
+                part = slice(LATE_GROUPS * a, LATE_GROUPS * (a + 1))
                 nc.sync.dma_start(out=w_late[:, part, :], in_=w_words[:, part, EARLY:DM])
 
-        early_banks = []
-        for y in range(PACK):
-            early_banks.append(psum.tile([P, EARLY], F32, tag="acc", name="early%d" % y))
+            def sort_x(s):
+                words = turn.tile([P, PACK * STEP_GROUPS, 2, P], F32, tag="x_sorted")
+                nc.vector.tensor_copy(
+                    out=words[:],
+                    in_=x_chunks[s][:].bitcast(F32).rearrange("x y (l r w) -> x (y l) w r", l=STEP_GROUPS, w=2),
+                )
+                x_sorted[s] = words
+                if s + LOADS_AHEAD < STEPS:
+                    load_x(s + LOADS_AHEAD)
 
-        transpose_x(0)
-        quantise_x(0)
-        for s in range(STEPS):
-            mask_in_sbuf(TILES // 2 + s)
-            row_maxima(s)
-            if s + 1 < STEPS:
-                transpose_x(s + 1)
-            for local in range(STEP_GROUPS):
-                for y in range(PACK):
-                    project(early_banks[y][:], STEP_GROUPS * s + local, y, w_chunks[s][:, local, :], slice(0, EARLY))
-            if s + 3 < STEPS:
-                load_step(s + 3)
-            if s + 3 == STEPS:
-                load_late()
-            exponentials(s)
-            if s + 1 < STEPS:
-                quantise_x(s + 1)
-
-        v_codes = keep.tile([P, H, DV], U32, align_bytes=64)
-        v_planes = keep.tile([P, H, DV], U8, align_bytes=64)
-        v_rounded = {}
-        v_grouped = {}
-
-        def round_values(h, y, product):
-            if y == 0:
-                v_rounded[h] = pair.tile([P, PACK, DV], BF16, tag="v_rounded", name="v_rounded%d" % h)
-            if y % 2 == 0:
-                nc.scalar.copy(out=v_rounded[h][:, y, :], in_=product)
-            else:
-                nc.vector.tensor_copy(out=v_rounded[h][:, y, :], in_=product)
-
-        def regroup_values(h):
-            grouped = pair.tile([P, DV, PACK], BF16, tag="v_grouped", align_bytes=64)
-            v_grouped[h] = grouped
-            nc.vector.tensor_copy(out=grouped[:], in_=v_rounded[h][:].rearrange("x y c -> x c y"))
-
-        def quantise_values(h):
-            nc.vector.quantize_mx(
-                out=v_codes[:, h, :].bitcast(FP8X4),
-                scales=v_planes[:, h, :],
-                in_=v_grouped[h][:].rearrange("x c y -> x (c y)"),
-            )
-
-        e_codes = keep.tile([P, H, N], U32, align_bytes=64)
-        e_planes = keep.tile([P, H, N], U8, align_bytes=64)
-        e_grouped = {}
-
-        def transpose_weights(h):
-            grouped = pair.tile([P, PACK, P, PACK], BF16, tag="e_grouped", align_bytes=64)
-            e_grouped[h] = grouped
-            for half in range(2):
-                bank = psum.tile([P, 2, PACK, P], BF16, tag="work")
-                for u in range(2):
-                    for y in range(PACK):
-                        nc.tensor.transpose(
-                            bank[:, u, y, :], weights[:, PACK * h + 2 * half + u, P * y : P * (y + 1)], ident_bf[:]
+            def transpose_x(s):
+                for local in range(STEP_GROUPS):
+                    grouped = turn.tile([P, N * PACK], BF16, tag="x_grouped", align_bytes=64)
+                    x_grouped[STEP_GROUPS * s + local] = grouped
+                    for half in range(2):
+                        bank = psum.tile([P, 2, 2, P], F32, tag="work")
+                        for y in range(2):
+                            for w in range(2):
+                                nc.tensor.transpose(
+                                    bank[:, w, y, :],
+                                    x_sorted[s][:, STEP_GROUPS * (2 * half + y) + local, w, :],
+                                    ident_f32[:],
+                                )
+                        nc.scalar.copy(
+                            out=grouped[:]
+                            .bitcast(F32)[:, N * half : N * (half + 1)]
+                            .rearrange("r (c w) -> r c w", w=2),
+                            in_=bank[:].rearrange("r w y x -> r (y x) w"),
                         )
-                target = grouped[:, 2 * half : 2 * half + 2, :, :]
-                source = bank[:].rearrange("z u y x -> z u x y")
+
+            def quantise_x(s):
+                for g in range(STEP_GROUPS * s, STEP_GROUPS * (s + 1)):
+                    nc.vector.quantize_mx(
+                        out=x_codes[:, g, :].bitcast(FP8X4), scales=x_planes[:, g, :], in_=x_grouped[g][:]
+                    )
+
+            for s in range(LOADS_AHEAD):
+                load_x(s)
+                load_w(s)
+
+            for h in range(H):
+                q_bank = psum.tile([P, PACK, P], BF16, tag="acc")
+                k_bank = psum.tile([P, PACK, P], BF16, tag="work")
+                for y in range(PACK):
+                    nc.tensor.transpose(q_bank[:, y, :], q_rows[:, h, y, :], ident_bf[:])
+                for y in range(PACK):
+                    nc.tensor.transpose(k_bank[:, y, :], k_rows[:, h, y, :], ident_bf[:])
+                nc.vector.tensor_copy(out=q_t[:, h], in_=q_bank[:])
+                nc.scalar.copy(out=k_t[:, h], in_=k_bank[:])
+
+            def score_bank(h, u, tag):
+                bank = psum.tile([P, N], F32, tag=tag)
+                nc.tensor.matmul(
+                    bank[:], lhsT=q_t[:, h, u, :], rhs=k_t[:, h].rearrange("d y z -> d (y z)"), start=True, stop=True
+                )
+                return bank
+
+            for h in range(H // 2):
+                for u in range(PACK):
+                    bank = score_bank(h, u, "acc")
+                    nc.vector.tensor_tensor(out=scores[:, PACK * h + u, :], in0=bank[:], in1=band_of(u), op=ALU.min)
+                    bank = score_bank(h + 2, u, "work")
+                    nc.scalar.copy(out=scores[:, PACK * (h + 2) + u, :], in_=bank[:])
+                sort_x(h)
+
+            for y in range(PACK):
+                early_banks.append(psum.tile([P, EARLY], F32, tag="acc", name="early%d" % y))
+            transpose_x(0)
+            quantise_x(0)
+            for s in range(STEPS):
+                row_maxima(s, 1)
+                if s + SORT_AHEAD < STEPS:
+                    sort_x(s + SORT_AHEAD)
+                if s + 1 < STEPS:
+                    transpose_x(s + 1)
+                for local in range(STEP_GROUPS):
+                    for y in range(PACK):
+                        project(
+                            early_banks[y][:], STEP_GROUPS * s + local, y, w_chunks[s][:, local, :], slice(0, EARLY)
+                        )
+                if s + LOADS_AHEAD < STEPS:
+                    load_w(s + LOADS_AHEAD)
+                if 0 <= s - LAST_X_STEP < GROUPS // LATE_GROUPS:
+                    load_late(s - LAST_X_STEP)
+                exponentials(s, 1)
+                if s + 1 < STEPS:
+                    quantise_x(s + 1)
+
+        with tc.tile_pool(name="late", bufs=1) as late:
+            v_rounded = late.tile([P, H, PACK, DV], BF16)
+            v_grouped = late.tile([P, H, DV, PACK], BF16, align_bytes=64)
+            e_grouped = late.tile([P, H, PACK, P, PACK], BF16, align_bytes=64)
+            e_banks = {}
+            result = late.tile([P, H, PACK, DV], F32)
+
+            def round_values(h, y, product):
+                nc.scalar.copy(out=v_rounded[:, h, y, :], in_=product)
+
+            def regroup_values(h):
+                nc.vector.tensor_copy(out=v_grouped[:, h], in_=v_rounded[:, h].rearrange("x y c -> x c y"))
+
+            def quantise_values(h):
+                nc.vector.quantize_mx(
+                    out=v_codes[:, h, :].bitcast(FP8X4),
+                    scales=v_planes[:, h, :],
+                    in_=v_grouped[:, h].rearrange("x c y -> x (c y)"),
+                )
+
+            def transpose_weights(h):
+                for half in range(2):
+                    bank = psum.tile([P, 2, PACK, P], BF16, tag="work")
+                    e_banks[(h, half)] = bank
+                    for u in range(2):
+                        for y in range(PACK):
+                            nc.tensor.transpose(
+                                bank[:, u, y, :], weights[:, PACK * h + 2 * half + u, P * y : P * (y + 1)], ident_bf[:]
+                            )
+
+            def regroup_weights(h, half):
+                target = e_grouped[:, h, 2 * half : 2 * half + 2, :, :]
+                source = e_banks[(h, half)][:].rearrange("z u y x -> z u x y")
                 if half == 0:
                     nc.scalar.copy(out=target, in_=source)
                 else:
                     nc.vector.tensor_copy(out=target, in_=source)
 
-        def quantise_weights(h):
-            nc.vector.quantize_mx(
-                out=e_codes[:, h, :].bitcast(FP8X4),
-                scales=e_planes[:, h, :],
-                in_=e_grouped[h][:].rearrange("z u x y -> z (u x y)"),
-            )
+            def quantise_weights(h):
+                nc.vector.quantize_mx(
+                    out=e_codes[:, h, :].bitcast(FP8X4),
+                    scales=e_planes[:, h, :],
+                    in_=e_grouped[:, h].rearrange("z u x y -> z (u x y)"),
+                )
 
-        def attend(h):
-            result = pair.tile([P, PACK, DV], F32, tag="result")
-            for half in range(2):
-                bank = psum.tile([P, 2, DV], F32, tag="work")
-                for local in range(2):
-                    queries = slice(P * (2 * half + local), P * (2 * half + local + 1))
-                    nc.tensor.matmul_mx(
-                        out=bank[:, local, :],
-                        lhsT=e_codes[:, h, queries].bitcast(FP8X4),
-                        lhsT_scale=e_planes[:, h, queries],
-                        rhs=v_codes[:, h, :].bitcast(FP8X4),
-                        rhs_scale=v_planes[:, h, :],
-                        start=True,
-                        stop=True,
-                    )
-                for local in range(2):
-                    u = 2 * half + local
-                    nc.scalar.activation(
-                        out=result[:, u, :],
-                        in_=bank[:, local, :],
-                        func=FUNC.Silu,
-                        scale=inv_den[:, PACK * h + u : PACK * h + u + 1],
-                    )
-                done = slice(2 * half, 2 * half + 2)
+            def attend(h):
                 rows = out[0, h].rearrange("(x u) c -> x u c", u=PACK)
-                nc.sync.dma_start(out=rows[:, done, :], in_=result[:, done, :])
+                for half in range(2):
+                    bank = psum.tile([P, 2, DV], F32, tag="work")
+                    for local in range(2):
+                        queries = slice(P * (2 * half + local), P * (2 * half + local + 1))
+                        nc.tensor.matmul_mx(
+                            out=bank[:, local, :],
+                            lhsT=e_codes[:, h, queries].bitcast(FP8X4),
+                            lhsT_scale=e_planes[:, h, queries],
+                            rhs=v_codes[:, h, :].bitcast(FP8X4),
+                            rhs_scale=v_planes[:, h, :],
+                            start=True,
+                            stop=True,
+                        )
+                    for local in range(2):
+                        u = 2 * half + local
+                        nc.scalar.activation(
+                            out=result[:, h, u, :],
+                            in_=bank[:, local, :],
+                            func=FUNC.Silu,
+                            scale=inv_den[:, PACK * h + u : PACK * h + u + 1],
+                        )
+                    done = slice(2 * half, 2 * half + 2)
+                    nc.sync.dma_start(out=rows[:, done, :], in_=result[:, h, done, :])
 
-        def project_late(h, y):
-            bank = psum.tile([P, DV], F32, tag="acc")
-            for g in range(GROUPS):
-                project(bank[:], g, y, w_late[:, g, DV * h - EARLY : DV * (h + 1) - EARLY], slice(DV * h, DV * (h + 1)))
-            round_values(h, y, bank[:])
+            def project_late(h, y):
+                bank = psum.tile([P, DV], F32, tag="acc")
+                of_head = slice(DV * h, DV * (h + 1))
+                for g in range(GROUPS):
+                    project(bank[:], g, y, w_late[:, g, DV * h - EARLY : DV * (h + 1) - EARLY], of_head)
+                round_values(h, y, bank[:])
 
-        for h in range(2):
             for y in range(PACK):
-                round_values(h, y, early_banks[y][:, DV * h : DV * (h + 1)])
-        transpose_weights(0)
-        transpose_weights(1)
-        regroup_values(0)
-        regroup_values(1)
-        quantise_weights(0)
-        quantise_weights(1)
-        quantise_values(0)
-        quantise_values(1)
-        denominators()
-        project_late(2, 0)
-        project_late(2, 1)
-        attend(0)
-        attend(1)
-        project_late(2, 2)
-        project_late(2, 3)
-        transpose_weights(2)
-        transpose_weights(3)
-        regroup_values(2)
-        quantise_weights(2)
-        quantise_weights(3)
-        quantise_values(2)
-        project_late(3, 0)
-        project_late(3, 1)
-        attend(2)
-        project_late(3, 2)
-        project_late(3, 3)
-        regroup_values(3)
-        quantise_values(3)
-        attend(3)
+                for h in range(2):
+                    round_values(h, y, early_banks[y][:, DV * h : DV * (h + 1)])
+            transpose_weights(0)
+            transpose_weights(1)
+            regroup_weights(0, 0)
+            regroup_weights(1, 0)
+            for y in range(PACK):
+                first = TILES // 2 + 2 * y
+                mask_in_sbuf(first)
+                mask_in_sbuf(first + 1)
+                row_maxima(first, 2)
+                exponentials(first, 2)
+                project_late(2, y)
+            regroup_weights(0, 1)
+            regroup_weights(1, 1)
+            regroup_values(0)
+            regroup_values(1)
+            quantise_weights(0)
+            quantise_weights(1)
+            quantise_values(0)
+            quantise_values(1)
+            transpose_weights(2)
+            transpose_weights(3)
+            regroup_weights(2, 0)
+            regroup_weights(3, 0)
+            regroup_weights(2, 1)
+            regroup_weights(3, 1)
+            project_late(3, 0)
+            denominators()
+            attend(0)
+            attend(1)
+            regroup_values(2)
+            quantise_weights(2)
+            quantise_weights(3)
+            quantise_values(2)
+            project_late(3, 1)
+            project_late(3, 2)
+            project_late(3, 3)
+            attend(2)
+            regroup_values(3)
+            quantise_values(3)
+            attend(3)

@@ -31,7 +31,6 @@ LOADS_AHEAD = 3
 SORT_AHEAD = 2
 LAST_X_STEP = STEPS - 1 - LOADS_AHEAD - SORT_AHEAD
 LATE_GROUPS = 4
-assert SORT_AHEAD == H // 2
 EARLY = 2 * DV
 TILES = H * PACK
 PLANES = 4
@@ -53,15 +52,18 @@ def tile_attention_pa_k_kernel(tc, q, k1, key_values_input, Wv1_words, Wv1_scale
 
         k_rows = keep.tile([P, H, PACK, DH], BF16)
         q_rows = keep.tile([P, H, PACK, DH], BF16)
-        for heads in (slice(0, 2), slice(2, H)):
-            nc.sync.dma_start(out=q_rows[:, heads], in_=q[0, heads].rearrange("h (x y) d -> x h y d", y=PACK))
-            nc.sync.dma_start(out=k_rows[:, heads], in_=k1[0, heads].rearrange("h (x y) d -> x h y d", y=PACK))
+
+        def load_qk(h):
+            nc.sync.dma_start(out=q_rows[:, h], in_=q[0, h].rearrange("(x y) d -> x y d", y=PACK))
+            nc.sync.dma_start(out=k_rows[:, h], in_=k1[0, h].rearrange("(x y) d -> x y d", y=PACK))
+
         sink_bf = keep.tile([P, H], BF16)
         nc.scalar.dma_start(out=sink_bf[:], in_=attn_sink.partition_broadcast(P))
 
         w_planes = keep.tile([P, GROUPS // PLANES, DM], U8, align_bytes=64)
         nc.vector.memset(w_planes[:].bitcast(I32), 0)
-        for a in range(GROUPS // PLANES):
+
+        def load_planes(a):
             for quadrant in range(4):
                 nc.sync.dma_start(
                     out=w_planes[32 * quadrant : 32 * quadrant + 4 * PLANES, a, :].bitcast(I32),
@@ -180,6 +182,8 @@ def tile_attention_pa_k_kernel(tc, q, k1, key_values_input, Wv1_words, Wv1_scale
                 x_chunks[s] = x_chunk
 
             def load_w(s):
+                if (STEP_GROUPS * s) % PLANES == 0:
+                    load_planes(STEP_GROUPS * s // PLANES)
                 w_chunk = stream.tile([P, STEP_GROUPS, EARLY], I32, align_bytes=64)
                 nc.sync.dma_start(out=w_chunk[:], in_=w_words[:, STEP_GROUPS * s : STEP_GROUPS * (s + 1), 0:EARLY])
                 w_chunks[s] = w_chunk
@@ -224,11 +228,17 @@ def tile_attention_pa_k_kernel(tc, q, k1, key_values_input, Wv1_words, Wv1_scale
                         out=x_codes[:, g, :].bitcast(FP8X4), scales=x_planes[:, g, :], in_=x_grouped[g][:]
                     )
 
-            for s in range(LOADS_AHEAD):
+            load_qk(0)
+            load_qk(2)
+            load_x(0)
+            load_qk(1)
+            load_qk(3)
+            load_w(0)
+            for s in range(1, LOADS_AHEAD):
                 load_x(s)
                 load_w(s)
 
-            for h in range(H):
+            def transpose_qk(h):
                 q_bank = psum.tile([P, PACK, P], BF16, tag="acc")
                 k_bank = psum.tile([P, PACK, P], BF16, tag="work")
                 for y in range(PACK):
@@ -245,18 +255,26 @@ def tile_attention_pa_k_kernel(tc, q, k1, key_values_input, Wv1_words, Wv1_scale
                 )
                 return bank
 
-            for h in range(H // 2):
+            def score_tiles(h):
                 for u in range(PACK):
                     bank = score_bank(h, u, "acc")
                     nc.vector.tensor_tensor(out=scores[:, PACK * h + u, :], in0=bank[:], in1=band_of(u), op=ALU.min)
                     bank = score_bank(h + 2, u, "work")
                     nc.scalar.copy(out=scores[:, PACK * (h + 2) + u, :], in_=bank[:])
-                sort_x(h)
+
+            transpose_qk(0)
+            transpose_qk(2)
+            sort_x(0)
+            score_tiles(0)
+            transpose_x(0)
+            transpose_qk(1)
+            transpose_qk(3)
+            score_tiles(1)
+            sort_x(1)
+            quantise_x(0)
 
             for y in range(PACK):
                 early_banks.append(psum.tile([P, EARLY], F32, tag="acc", name="early%d" % y))
-            transpose_x(0)
-            quantise_x(0)
             for s in range(STEPS):
                 row_maxima(s, 1)
                 if s + SORT_AHEAD < STEPS:
@@ -347,12 +365,14 @@ def tile_attention_pa_k_kernel(tc, q, k1, key_values_input, Wv1_words, Wv1_scale
                     done = slice(2 * half, 2 * half + 2)
                     nc.sync.dma_start(out=rows[:, done, :], in_=result[:, h, done, :])
 
-            def project_late(h, y):
+            def project_late(bank, h, y, g):
+                project(bank, g, y, w_late[:, g, DV * h - EARLY : DV * (h + 1) - EARLY], slice(DV * h, DV * (h + 1)))
+
+            def last_head(y):
                 bank = psum.tile([P, DV], F32, tag="acc")
-                of_head = slice(DV * h, DV * (h + 1))
                 for g in range(GROUPS):
-                    project(bank[:], g, y, w_late[:, g, DV * h - EARLY : DV * (h + 1) - EARLY], of_head)
-                round_values(h, y, bank[:])
+                    project_late(bank[:], H - 1, y, g)
+                round_values(H - 1, y, bank[:])
 
             for y in range(PACK):
                 for h in range(2):
@@ -361,13 +381,20 @@ def tile_attention_pa_k_kernel(tc, q, k1, key_values_input, Wv1_words, Wv1_scale
             transpose_weights(1)
             regroup_weights(0, 0)
             regroup_weights(1, 0)
+            banks_2 = []
             for y in range(PACK):
-                first = TILES // 2 + 2 * y
+                banks_2.append(psum.tile([P, DV], F32, tag="acc", name="head2_%d" % y))
+            for a in range(GROUPS // LATE_GROUPS):
+                first = TILES // 2 + 2 * a
                 mask_in_sbuf(first)
                 mask_in_sbuf(first + 1)
                 row_maxima(first, 2)
                 exponentials(first, 2)
-                project_late(2, y)
+                for g in range(LATE_GROUPS * a, LATE_GROUPS * (a + 1)):
+                    for y in range(PACK):
+                        project_late(banks_2[y][:], 2, y, g)
+            for y in range(PACK):
+                round_values(2, y, banks_2[y][:])
             regroup_weights(0, 1)
             regroup_weights(1, 1)
             regroup_values(0)
@@ -382,7 +409,7 @@ def tile_attention_pa_k_kernel(tc, q, k1, key_values_input, Wv1_words, Wv1_scale
             regroup_weights(3, 0)
             regroup_weights(2, 1)
             regroup_weights(3, 1)
-            project_late(3, 0)
+            last_head(0)
             denominators()
             attend(0)
             attend(1)
@@ -390,9 +417,9 @@ def tile_attention_pa_k_kernel(tc, q, k1, key_values_input, Wv1_words, Wv1_scale
             quantise_weights(2)
             quantise_weights(3)
             quantise_values(2)
-            project_late(3, 1)
-            project_late(3, 2)
-            project_late(3, 3)
+            last_head(1)
+            last_head(2)
+            last_head(3)
             attend(2)
             regroup_values(3)
             quantise_values(3)

@@ -29,7 +29,6 @@ STEPS = GROUPS // STEP_GROUPS
 CHUNK = STEP_GROUPS * K_PASS
 LOADS_AHEAD = 3
 SORT_AHEAD = 2
-LAST_X_STEP = STEPS - 1 - LOADS_AHEAD - SORT_AHEAD
 LATE_GROUPS = 4
 EARLY = 2 * DV
 TILES = H * PACK
@@ -188,9 +187,14 @@ def tile_attention_pa_k_kernel(tc, q, k1, key_values_input, Wv1_words, Wv1_scale
                 nc.sync.dma_start(out=w_chunk[:], in_=w_words[:, STEP_GROUPS * s : STEP_GROUPS * (s + 1), 0:EARLY])
                 w_chunks[s] = w_chunk
 
-            def load_late(a):
-                part = slice(LATE_GROUPS * a, LATE_GROUPS * (a + 1))
-                nc.sync.dma_start(out=w_late[:, part, :], in_=w_words[:, part, EARLY:DM])
+            def load_step(s):
+                if s + 1 < STEPS:
+                    load_x(s + 1)
+                load_w(s)
+                if s == STEPS - 1:
+                    for a in range(GROUPS // LATE_GROUPS):
+                        part = slice(LATE_GROUPS * a, LATE_GROUPS * (a + 1))
+                        nc.sync.dma_start(out=w_late[:, part, :], in_=w_words[:, part, EARLY:DM])
 
             def sort_x(s):
                 words = turn.tile([P, PACK * STEP_GROUPS, 2, P], F32, tag="x_sorted")
@@ -199,8 +203,6 @@ def tile_attention_pa_k_kernel(tc, q, k1, key_values_input, Wv1_words, Wv1_scale
                     in_=x_chunks[s][:].bitcast(F32).rearrange("x y (l r w) -> x (y l) w r", l=STEP_GROUPS, w=2),
                 )
                 x_sorted[s] = words
-                if s + LOADS_AHEAD < STEPS:
-                    load_x(s + LOADS_AHEAD)
 
             def transpose_x(s):
                 for local in range(STEP_GROUPS):
@@ -233,10 +235,8 @@ def tile_attention_pa_k_kernel(tc, q, k1, key_values_input, Wv1_words, Wv1_scale
             load_x(0)
             load_qk(1)
             load_qk(3)
-            load_w(0)
-            for s in range(1, LOADS_AHEAD):
-                load_x(s)
-                load_w(s)
+            for s in range(LOADS_AHEAD - 1):
+                load_step(s)
 
             def transpose_qk(h):
                 q_bank = psum.tile([P, PACK, P], BF16, tag="acc")
@@ -265,12 +265,13 @@ def tile_attention_pa_k_kernel(tc, q, k1, key_values_input, Wv1_words, Wv1_scale
             transpose_qk(0)
             transpose_qk(2)
             sort_x(0)
+            load_step(LOADS_AHEAD - 1)
             score_tiles(0)
+            sort_x(1)
             transpose_x(0)
             transpose_qk(1)
             transpose_qk(3)
             score_tiles(1)
-            sort_x(1)
             quantise_x(0)
 
             for y in range(PACK):
@@ -287,9 +288,7 @@ def tile_attention_pa_k_kernel(tc, q, k1, key_values_input, Wv1_words, Wv1_scale
                             early_banks[y][:], STEP_GROUPS * s + local, y, w_chunks[s][:, local, :], slice(0, EARLY)
                         )
                 if s + LOADS_AHEAD < STEPS:
-                    load_w(s + LOADS_AHEAD)
-                if 0 <= s - LAST_X_STEP < GROUPS // LATE_GROUPS:
-                    load_late(s - LAST_X_STEP)
+                    load_step(s + LOADS_AHEAD)
                 exponentials(s, 1)
                 if s + 1 < STEPS:
                     quantise_x(s + 1)

@@ -90,7 +90,10 @@ def tile_attention_pa_k_kernel(tc, q, k1, key_values_input, Wv1_words, Wv1_scale
         masks.make_identity(nc, ident_f32[:])
 
         def band_of(u):
-            return band[:, PACK - 1 - u : 2 * PACK - 1 - u, :].rearrange("x a z -> x (a z)")
+            return band[:, PACK - 1 - u : 2 * PACK - 1 - u, :].rearrange("x (w e) z -> x w z e", e=2)
+
+        def by_pair(tile_columns):
+            return tile_columns.rearrange("x (w z e) -> x w z e", w=2, e=2)
 
         warm = keep.tile([P, 1], F32)
         nc.vector.memset(warm[:], 0.0)
@@ -111,7 +114,9 @@ def tile_attention_pa_k_kernel(tc, q, k1, key_values_input, Wv1_words, Wv1_scale
         inv_den = keep.tile([P, TILES], F32)
 
         def mask_in_sbuf(i):
-            nc.vector.tensor_tensor(out=scores[:, i, :], in0=scores[:, i, :], in1=band_of(i % PACK), op=ALU.min)
+            nc.vector.tensor_tensor(
+                out=by_pair(scores[:, i, :]), in0=by_pair(scores[:, i, :]), in1=band_of(i % PACK), op=ALU.min
+            )
 
         def row_maxima(first, count):
             h = first // PACK
@@ -154,7 +159,7 @@ def tile_attention_pa_k_kernel(tc, q, k1, key_values_input, Wv1_words, Wv1_scale
         e_codes = keep.tile([P, H, N], U32, align_bytes=64)
         e_planes = keep.tile([P, H, N], U8, align_bytes=64)
         q_t = keep.tile([P, H, PACK, P], BF16)
-        k_t = keep.tile([P, H, PACK, P], BF16)
+        k_t = keep.tile([P, H, N], BF16)
 
         def project(bank, g, y, w_codes, columns):
             tokens = slice(P * y, P * (y + 1))
@@ -246,19 +251,24 @@ def tile_attention_pa_k_kernel(tc, q, k1, key_values_input, Wv1_words, Wv1_scale
                 for y in range(PACK):
                     nc.tensor.transpose(k_bank[:, y, :], k_rows[:, h, y, :], ident_bf[:])
                 nc.vector.tensor_copy(out=q_t[:, h], in_=q_bank[:])
-                nc.scalar.copy(out=k_t[:, h], in_=k_bank[:])
+                nc.scalar.copy(
+                    out=k_t[:, h].rearrange("d (w z e) -> d w z e", w=2, e=2),
+                    in_=k_bank[:].rearrange("d (w e) z -> d w z e", e=2),
+                )
 
             def score_bank(h, u, tag):
                 bank = psum.tile([P, N], F32, tag=tag)
                 nc.tensor.matmul(
-                    bank[:], lhsT=q_t[:, h, u, :], rhs=k_t[:, h].rearrange("d y z -> d (y z)"), start=True, stop=True
+                    bank[:], lhsT=q_t[:, h, u, :], rhs=k_t[:, h], start=True, stop=True
                 )
                 return bank
 
             def score_tiles(h):
                 for u in range(PACK):
                     bank = score_bank(h, u, "acc")
-                    nc.vector.tensor_tensor(out=scores[:, PACK * h + u, :], in0=bank[:], in1=band_of(u), op=ALU.min)
+                    nc.vector.tensor_tensor(
+                        out=by_pair(scores[:, PACK * h + u, :]), in0=by_pair(bank[:]), in1=band_of(u), op=ALU.min
+                    )
                     bank = score_bank(h + 2, u, "work")
                     nc.scalar.copy(out=scores[:, PACK * (h + 2) + u, :], in_=bank[:])
 
@@ -315,17 +325,21 @@ def tile_attention_pa_k_kernel(tc, q, k1, key_values_input, Wv1_words, Wv1_scale
 
             def transpose_weights(h):
                 for half in range(2):
-                    bank = psum.tile([P, 2, PACK, P], BF16, tag="work")
+                    bank = psum.tile([P, 2, 2, P], F32, tag="work")
                     e_banks[(h, half)] = bank
                     for u in range(2):
-                        for y in range(PACK):
-                            nc.tensor.transpose(
-                                bank[:, u, y, :], weights[:, PACK * h + 2 * half + u, P * y : P * (y + 1)], ident_bf[:]
-                            )
+                        words = weights[:, PACK * h + 2 * half + u, :].bitcast(F32)
+                        for w in range(2):
+                            nc.tensor.transpose(bank[:, u, w, :], words[:, P * w : P * (w + 1)], ident_f32[:])
 
             def regroup_weights(h, half):
-                target = e_grouped[:, h, 2 * half : 2 * half + 2, :, :]
-                source = e_banks[(h, half)][:].rearrange("z u y x -> z u x y")
+                target = (
+                    e_grouped[:, h, 2 * half : 2 * half + 2, :, :]
+                    .rearrange("z u x y -> z (u x y)")
+                    .bitcast(F32)
+                    .rearrange("z (u x w) -> z u x w", u=2, w=2)
+                )
+                source = e_banks[(h, half)][:].rearrange("z u w x -> z u x w")
                 if half == 0:
                     nc.scalar.copy(out=target, in_=source)
                 else:

@@ -33,6 +33,7 @@ LATE_GROUPS = 4
 EARLY = 2 * DV
 TILES = H * PACK
 PLANES = 4
+WARM_UP = 4
 SCALE = DH ** -0.5
 BIG = 3.4028234663852886e38
 
@@ -49,12 +50,18 @@ def tile_attention_pa_k_kernel(tc, q, k1, key_values_input, Wv1_words, Wv1_scale
         x_rows = key_values_input[0].rearrange("(x y) k -> x y k", y=PACK)
         w_words = Wv1_words.rearrange("g r n t -> g r (n t)").bitcast(I32).rearrange("g r n -> r g n")
 
+        zeros = keep.tile([P, N], BF16)
+        nc.vector.memset(zeros[:], 0.0)
+        idle_bank = psum.tile([P, N], F32, tag="work")
+        for i in range(WARM_UP):
+            nc.tensor.matmul(idle_bank[:], lhsT=zeros[:, 0:P], rhs=zeros[:], start=True, stop=True)
+
         k_rows = keep.tile([P, H, PACK, DH], BF16)
         q_rows = keep.tile([P, H, PACK, DH], BF16)
 
         def load_qk(h):
-            nc.sync.dma_start(out=q_rows[:, h], in_=q[0, h].rearrange("(x y) d -> x y d", y=PACK))
-            nc.sync.dma_start(out=k_rows[:, h], in_=k1[0, h].rearrange("(x y) d -> x y d", y=PACK))
+            nc.sync.dma_start(out=q_rows[:, h:H:2], in_=q[0, h:H:2].rearrange("h (x y) d -> x h y d", y=PACK))
+            nc.sync.dma_start(out=k_rows[:, h:H:2], in_=k1[0, h:H:2].rearrange("h (x y) d -> x h y d", y=PACK))
 
         sink_bf = keep.tile([P, H], BF16)
         nc.scalar.dma_start(out=sink_bf[:], in_=attn_sink.partition_broadcast(P))
@@ -236,10 +243,8 @@ def tile_attention_pa_k_kernel(tc, q, k1, key_values_input, Wv1_words, Wv1_scale
                     )
 
             load_qk(0)
-            load_qk(2)
             load_x(0)
             load_qk(1)
-            load_qk(3)
             for s in range(LOADS_AHEAD - 1):
                 load_step(s)
 
@@ -387,6 +392,55 @@ def tile_attention_pa_k_kernel(tc, q, k1, key_values_input, Wv1_words, Wv1_scale
                     project_late(bank[:], H - 1, y, g)
                 round_values(H - 1, y, bank[:])
 
+            HALF = DV // 2
+
+            def last_product_half(part):
+                h = H - 1
+                y = PACK - 1
+                bank = psum.tile([P, HALF], F32, tag="acc")
+                first = DV * h + HALF * part
+                for g in range(GROUPS):
+                    project(bank[:], g, y, w_late[:, g, first - EARLY : first - EARLY + HALF], slice(first, first + HALF))
+                nc.scalar.copy(out=v_rounded[:, h, y, HALF * part : HALF * (part + 1)], in_=bank[:])
+
+            def finish_values_half(part):
+                h = H - 1
+                columns = slice(HALF * part, HALF * (part + 1))
+                nc.vector.tensor_copy(
+                    out=v_grouped[:, h, columns, :], in_=v_rounded[:, h, :, columns].rearrange("x y c -> x c y")
+                )
+                nc.vector.quantize_mx(
+                    out=v_codes[:, h, columns].bitcast(FP8X4),
+                    scales=v_planes[:, h, columns],
+                    in_=v_grouped[:, h, columns, :].rearrange("x c y -> x (c y)"),
+                )
+
+            def attend_half(part):
+                h = H - 1
+                columns = slice(HALF * part, HALF * (part + 1))
+                bank = psum.tile([P, PACK, HALF], F32, tag="work")
+                for u in range(PACK):
+                    queries = slice(P * u, P * (u + 1))
+                    nc.tensor.matmul_mx(
+                        out=bank[:, u, :],
+                        lhsT=e_codes[:, h, queries].bitcast(FP8X4),
+                        lhsT_scale=e_planes[:, h, queries],
+                        rhs=v_codes[:, h, columns].bitcast(FP8X4),
+                        rhs_scale=v_planes[:, h, columns],
+                        start=True,
+                        stop=True,
+                    )
+                for u in range(PACK):
+                    nc.scalar.activation(
+                        out=result[:, h, u, columns],
+                        in_=bank[:, u, :],
+                        func=FUNC.Silu,
+                        scale=inv_den[:, PACK * h + u : PACK * h + u + 1],
+                    )
+                nc.sync.dma_start(
+                    out=out[0, h].rearrange("(x u) c -> x u c", u=PACK)[:, :, columns], in_=result[:, h, :, columns]
+                )
+
             for y in range(PACK):
                 for h in range(2):
                     round_values(h, y, early_banks[y][:, DV * h : DV * (h + 1)])
@@ -432,8 +486,10 @@ def tile_attention_pa_k_kernel(tc, q, k1, key_values_input, Wv1_words, Wv1_scale
             quantise_values(2)
             last_head(1)
             last_head(2)
-            last_head(3)
+            last_product_half(0)
+            finish_values_half(0)
             attend(2)
-            regroup_values(3)
-            quantise_values(3)
-            attend(3)
+            last_product_half(1)
+            finish_values_half(1)
+            attend_half(0)
+            attend_half(1)

@@ -282,10 +282,10 @@ def tile_attention_pa_k_kernel(tc, q, k1, key_values_input, Wv1_words, Wv1_scale
             sort_x(0)
             load_step(LOADS_AHEAD - 1)
             score_tiles(0)
-            sort_x(1)
-            transpose_x(0)
             transpose_qk(1)
             transpose_qk(3)
+            sort_x(1)
+            transpose_x(0)
             score_tiles(1)
             quantise_x(0)
 

@@ -401,14 +401,17 @@ def tile_attention_pa_k_kernel(tc, q, k1, key_values_input, Wv1_words, Wv1_scale
                 first = DV * h + HALF * part
                 for g in range(GROUPS):
                     project(bank[:], g, y, w_late[:, g, first - EARLY : first - EARLY + HALF], slice(first, first + HALF))
-                nc.scalar.copy(out=v_rounded[:, h, y, HALF * part : HALF * (part + 1)], in_=bank[:])
+                nc.vector.tensor_copy(out=v_grouped[:, h, HALF * part : HALF * (part + 1), y], in_=bank[:])
+
+            def regroup_first_three():
+                h = H - 1
+                nc.vector.tensor_copy(
+                    out=v_grouped[:, h, :, 0 : PACK - 1], in_=v_rounded[:, h, 0 : PACK - 1, :].rearrange("x y c -> x c y")
+                )
 
             def finish_values_half(part):
                 h = H - 1
                 columns = slice(HALF * part, HALF * (part + 1))
-                nc.vector.tensor_copy(
-                    out=v_grouped[:, h, columns, :], in_=v_rounded[:, h, :, columns].rearrange("x y c -> x c y")
-                )
                 nc.vector.quantize_mx(
                     out=v_codes[:, h, columns].bitcast(FP8X4),
                     scales=v_planes[:, h, columns],
@@ -430,6 +433,7 @@ def tile_attention_pa_k_kernel(tc, q, k1, key_values_input, Wv1_words, Wv1_scale
                         start=True,
                         stop=True,
                     )
+                rows = out[0, h].rearrange("(x u) c -> x u c", u=PACK)
                 for u in range(PACK):
                     nc.scalar.activation(
                         out=result[:, h, u, columns],
@@ -437,9 +441,10 @@ def tile_attention_pa_k_kernel(tc, q, k1, key_values_input, Wv1_words, Wv1_scale
                         func=FUNC.Silu,
                         scale=inv_den[:, PACK * h + u : PACK * h + u + 1],
                     )
-                nc.sync.dma_start(
-                    out=out[0, h].rearrange("(x u) c -> x u c", u=PACK)[:, :, columns], in_=result[:, h, :, columns]
-                )
+                    if part == 1:
+                        nc.sync.dma_start(out=rows[:, u, columns], in_=result[:, h, u, columns])
+                if part == 0:
+                    nc.sync.dma_start(out=rows[:, :, columns], in_=result[:, h, :, columns])
 
             for y in range(PACK):
                 for h in range(2):
@@ -457,8 +462,8 @@ def tile_attention_pa_k_kernel(tc, q, k1, key_values_input, Wv1_words, Wv1_scale
                 mask_in_sbuf(first + 1)
                 row_maxima(first, 2)
                 exponentials(first, 2)
-                for g in range(LATE_GROUPS * a, LATE_GROUPS * (a + 1)):
-                    for y in range(PACK):
+                for y in range(PACK):
+                    for g in range(LATE_GROUPS * a, LATE_GROUPS * (a + 1)):
                         project_late(banks_2[y][:], 2, y, g)
             for y in range(PACK):
                 round_values(2, y, banks_2[y][:])
@@ -486,6 +491,7 @@ def tile_attention_pa_k_kernel(tc, q, k1, key_values_input, Wv1_words, Wv1_scale
             quantise_values(2)
             last_head(1)
             last_head(2)
+            regroup_first_three()
             last_product_half(0)
             finish_values_half(0)
             attend(2)

@@ -69,11 +69,11 @@ def tile_attention_pa_k_kernel(tc, q, k1, key_values_input, Wv1_words, Wv1_scale
         w_planes = keep.tile([P, GROUPS // PLANES, DM], U8, align_bytes=64)
         nc.vector.memset(w_planes[:].bitcast(I32), 0)
 
-        def load_planes(a):
+        def load_planes(a, columns):
             for quadrant in range(4):
                 nc.sync.dma_start(
-                    out=w_planes[32 * quadrant : 32 * quadrant + 4 * PLANES, a, :].bitcast(I32),
-                    in_=Wv1_scales[PLANES * a : PLANES * (a + 1), 4 * quadrant : 4 * quadrant + 4, :].bitcast(I32),
+                    out=w_planes[32 * quadrant : 32 * quadrant + 4 * PLANES, a, columns].bitcast(I32),
+                    in_=Wv1_scales[PLANES * a : PLANES * (a + 1), 4 * quadrant : 4 * quadrant + 4, columns].bitcast(I32),
                 )
 
         def w_plane(g, columns):
@@ -194,7 +194,7 @@ def tile_attention_pa_k_kernel(tc, q, k1, key_values_input, Wv1_words, Wv1_scale
 
             def load_w(s):
                 if (STEP_GROUPS * s) % PLANES == 0:
-                    load_planes(STEP_GROUPS * s // PLANES)
+                    load_planes(STEP_GROUPS * s // PLANES, slice(0, EARLY))
                 w_chunk = stream.tile([P, STEP_GROUPS, EARLY], I32, align_bytes=64)
                 nc.sync.dma_start(out=w_chunk[:], in_=w_words[:, STEP_GROUPS * s : STEP_GROUPS * (s + 1), 0:EARLY])
                 w_chunks[s] = w_chunk
@@ -204,6 +204,8 @@ def tile_attention_pa_k_kernel(tc, q, k1, key_values_input, Wv1_words, Wv1_scale
                     load_x(s + 1)
                 load_w(s)
                 if s == STEPS - 1:
+                    for a in range(GROUPS // PLANES):
+                        load_planes(a, slice(EARLY, DM))
                     for a in range(GROUPS // LATE_GROUPS):
                         part = slice(LATE_GROUPS * a, LATE_GROUPS * (a + 1))
                         nc.sync.dma_start(out=w_late[:, part, :], in_=w_words[:, part, EARLY:DM])

@@ -34,6 +34,7 @@ EARLY = 2 * DV
 TILES = H * PACK
 PLANES = 4
 WARM_UP = 4
+MASKED_AT_ONCE = (TILES - 1,)
 SCALE = DH ** -0.5
 BIG = 3.4028234663852886e38
 
@@ -121,6 +122,8 @@ def tile_attention_pa_k_kernel(tc, q, k1, key_values_input, Wv1_words, Wv1_scale
         inv_den = keep.tile([P, TILES], F32)
 
         def mask_in_sbuf(i):
+            if i in MASKED_AT_ONCE:
+                return
             nc.vector.tensor_tensor(
                 out=by_pair(scores[:, i, :]), in0=by_pair(scores[:, i, :]), in1=band_of(i % PACK), op=ALU.min
             )
@@ -196,7 +199,11 @@ def tile_attention_pa_k_kernel(tc, q, k1, key_values_input, Wv1_words, Wv1_scale
                 if (STEP_GROUPS * s) % PLANES == 0:
                     load_planes(STEP_GROUPS * s // PLANES, slice(0, EARLY))
                 w_chunk = stream.tile([P, STEP_GROUPS, EARLY], I32, align_bytes=64)
-                nc.sync.dma_start(out=w_chunk[:], in_=w_words[:, STEP_GROUPS * s : STEP_GROUPS * (s + 1), 0:EARLY])
+                if s == 0:
+                    for local in range(STEP_GROUPS):
+                        nc.sync.dma_start(out=w_chunk[:, local, :], in_=w_words[:, local, 0:EARLY])
+                else:
+                    nc.sync.dma_start(out=w_chunk[:], in_=w_words[:, STEP_GROUPS * s : STEP_GROUPS * (s + 1), 0:EARLY])
                 w_chunks[s] = w_chunk
 
             def load_step(s):
@@ -277,7 +284,12 @@ def tile_attention_pa_k_kernel(tc, q, k1, key_values_input, Wv1_words, Wv1_scale
                         out=by_pair(scores[:, PACK * h + u, :]), in0=by_pair(bank[:]), in1=band_of(u), op=ALU.min
                     )
                     bank = score_bank(h + 2, u, "work")
-                    nc.scalar.copy(out=scores[:, PACK * (h + 2) + u, :], in_=bank[:])
+                    if PACK * (h + 2) + u in MASKED_AT_ONCE:
+                        nc.vector.tensor_tensor(
+                            out=by_pair(scores[:, PACK * (h + 2) + u, :]), in0=by_pair(bank[:]), in1=band_of(u), op=ALU.min
+                        )
+                    else:
+                        nc.scalar.copy(out=scores[:, PACK * (h + 2) + u, :], in_=bank[:])
 
             transpose_qk(0)
             transpose_qk(2)
@@ -423,11 +435,12 @@ def tile_attention_pa_k_kernel(tc, q, k1, key_values_input, Wv1_words, Wv1_scale
             def attend_half(part):
                 h = H - 1
                 columns = slice(HALF * part, HALF * (part + 1))
-                bank = psum.tile([P, PACK, HALF], F32, tag="work")
+                banks = []
                 for u in range(PACK):
+                    banks.append(psum.tile([P, HALF], F32, tag="work", name="last%d" % u))
                     queries = slice(P * u, P * (u + 1))
                     nc.tensor.matmul_mx(
-                        out=bank[:, u, :],
+                        out=banks[u][:],
                         lhsT=e_codes[:, h, queries].bitcast(FP8X4),
                         lhsT_scale=e_planes[:, h, queries],
                         rhs=v_codes[:, h, columns].bitcast(FP8X4),
@@ -439,7 +452,7 @@ def tile_attention_pa_k_kernel(tc, q, k1, key_values_input, Wv1_words, Wv1_scale
                 for u in range(PACK):
                     nc.scalar.activation(
                         out=result[:, h, u, columns],
-                        in_=bank[:, u, :],
+                        in_=banks[u][:],
                         func=FUNC.Silu,
                         scale=inv_den[:, PACK * h + u : PACK * h + u + 1],
                     )

from contextlib import ExitStack

import concourse.masks as masks
import concourse.mybir as mybir

BF16 = mybir.dt.bfloat16
F32 = mybir.dt.float32
I32 = mybir.dt.int32
U32 = mybir.dt.uint32
U8 = mybir.dt.uint8
FP8X4 = mybir.dt.float8_e4m3fn_x4
ALU = mybir.AluOpType
FUNC = mybir.ActivationFunctionType
AXIS = mybir.AxisListType

P = 128
PACK = 4
K_PASS = P * PACK
N = 512
H = 4
DH = 128
DV = 256
DKV = 8192
DM = H * DV
WINDOW = 256
GROUPS = DKV // K_PASS
STEP_GROUPS = 2
STEPS = GROUPS // STEP_GROUPS
CHUNK = STEP_GROUPS * K_PASS
LOADS_AHEAD = 3
SORT_AHEAD = 2
LATE_GROUPS = 4
EARLY = 2 * DV
TILES = H * PACK
PLANES = 4
WARM_UP = 4
MASKED_AT_ONCE = (TILES - 1,)
SCALE = DH ** -0.5
BIG = 3.4028234663852886e38

FLOPS = 2 * N * DKV * DM + H * (2 * N * N * DH + 2 * N * N * DV)


def tile_attention_pa_k_kernel(tc, q, k1, key_values_input, Wv1_words, Wv1_scales, attn_sink, out):
    nc = tc.nc
    with ExitStack() as ctx:
        ctx.enter_context(tc.manual_schedule())
        keep = ctx.enter_context(tc.tile_pool(name="keep", bufs=1))
        psum = ctx.enter_context(tc.psum_pool(name="psum", bufs=4))

        x_rows = key_values_input[0].rearrange("(x y) k -> x y k", y=PACK)
        w_words = Wv1_words.rearrange("g r n t -> g r (n t)").bitcast(I32).rearrange("g r n -> r g n")

        zeros = keep.tile([P, N], BF16)
        nc.vector.memset(zeros[:], 0.0)
        idle_bank = psum.tile([P, N], F32, tag="work")
        for i in range(WARM_UP):
            nc.tensor.matmul(idle_bank[:], lhsT=zeros[:, 0:P], rhs=zeros[:], start=True, stop=True)

        k_rows = keep.tile([P, H, PACK, DH], BF16)
        q_rows = keep.tile([P, H, PACK, DH], BF16)

        def load_qk(h):
            nc.sync.dma_start(out=q_rows[:, h:H:2], in_=q[0, h:H:2].rearrange("h (x y) d -> x h y d", y=PACK))
            nc.sync.dma_start(out=k_rows[:, h:H:2], in_=k1[0, h:H:2].rearrange("h (x y) d -> x h y d", y=PACK))

        sink_bf = keep.tile([P, H], BF16)
        nc.scalar.dma_start(out=sink_bf[:], in_=attn_sink.partition_broadcast(P))

        w_planes = keep.tile([P, GROUPS // PLANES, DM], U8, align_bytes=64)
        nc.vector.memset(w_planes[:].bitcast(I32), 0)

        def load_planes(a, columns):
            for quadrant in range(4):
                nc.sync.dma_start(
                    out=w_planes[32 * quadrant : 32 * quadrant + 4 * PLANES, a, columns].bitcast(I32),
                    in_=Wv1_scales[PLANES * a : PLANES * (a + 1), 4 * quadrant : 4 * quadrant + 4, columns].bitcast(I32),
                )

        def w_plane(g, columns):
            return w_planes[4 * (g % PLANES) : P, g // PLANES, columns]

        band = keep.tile([P, 2 * PACK - 1, P], F32)
        nc.vector.memset(band[:], BIG)
        ident_bf = keep.tile([P, P], BF16)
        masks.make_identity(nc, ident_bf[:])
        for base, fill in ((PACK - 1, -BIG), (WINDOW + PACK - 1, BIG)):
            nc.gpsimd.affine_select(
                out=band[:],
                in_=band[:],
                pattern=[[-1, 2 * PACK - 1], [-PACK, P]],
                compare_op=ALU.is_ge,
                fill=fill,
                base=base,
                channel_multiplier=PACK,
            )
        ident_f32 = keep.tile([P, P], F32)
        masks.make_identity(nc, ident_f32[:])

        def band_of(u):
            return band[:, PACK - 1 - u : 2 * PACK - 1 - u, :].rearrange("x (w e) z -> x w z e", e=2)

        def by_pair(tile_columns):
            return tile_columns.rearrange("x (w z e) -> x w z e", w=2, e=2)

        warm = keep.tile([P, 1], F32)
        nc.vector.memset(warm[:], 0.0)
        nc.scalar.activation(out=warm[:], in_=warm[:], func=FUNC.Exp)

        sink = keep.tile([P, H], F32)
        nc.vector.tensor_copy(out=sink[:], in_=sink_bf[:])
        neg_sink = keep.tile([P, H], F32)
        nc.vector.tensor_scalar_mul(out=neg_sink[:], in0=sink_bf[:], scalar1=-1.0)

        scores = keep.tile([P, TILES, N], F32)
        weights = keep.tile([P, TILES, N], BF16)
        row_max = keep.tile([P, TILES], F32)
        neg_max = keep.tile([P, TILES], F32)
        row_sum = keep.tile([P, TILES], F32)
        sink_term = keep.tile([P, TILES], F32)
        denominator = keep.tile([P, TILES], F32)
        inv_den = keep.tile([P, TILES], F32)

        def mask_in_sbuf(i):
            if i in MASKED_AT_ONCE:
                return
            nc.vector.tensor_tensor(
                out=by_pair(scores[:, i, :]), in0=by_pair(scores[:, i, :]), in1=band_of(i % PACK), op=ALU.min
            )

        def row_maxima(first, count):
            h = first // PACK
            these = slice(first, first + count)
            nc.vector.tensor_reduce(out=row_max[:, these], in_=scores[:, these, :], axis=AXIS.X, op=ALU.max)
            nc.vector.tensor_scalar(
                out=neg_max[:, these],
                in0=row_max[:, these],
                scalar1=-SCALE,
                scalar2=neg_sink[:, h : h + 1],
                op0=ALU.mult,
                op1=ALU.min,
            )

        def exponentials(first, count):
            for i in range(first, first + count):
                nc.scalar.activation(
                    out=weights[:, i, :],
                    in_=scores[:, i, :],
                    func=FUNC.Exp,
                    bias=neg_max[:, i : i + 1],
                    scale=SCALE,
                    accum_out=row_sum[:, i : i + 1],
                )

        def denominators():
            for h in range(H):
                of_head = slice(PACK * h, PACK * (h + 1))
                nc.scalar.activation(
                    out=sink_term[:, of_head], in_=neg_max[:, of_head], func=FUNC.Exp, bias=sink[:, h : h + 1]
                )
            nc.vector.tensor_tensor(out=denominator[:], in0=row_sum[:], in1=sink_term[:], op=ALU.add)
            nc.vector.reciprocal(out=inv_den[:], in_=denominator[:])

        x_codes = keep.tile([P, GROUPS, N], U32, align_bytes=64)
        x_planes = keep.tile([P, GROUPS, N], U8, align_bytes=64)
        w_late = keep.tile([P, GROUPS, DM - EARLY], I32, align_bytes=64)
        v_codes = keep.tile([P, H, DV], U32, align_bytes=64)
        v_planes = keep.tile([P, H, DV], U8, align_bytes=64)
        e_codes = keep.tile([P, H, N], U32, align_bytes=64)
        e_planes = keep.tile([P, H, N], U8, align_bytes=64)
        q_t = keep.tile([P, H, PACK, P], BF16)
        k_t = keep.tile([P, H, N], BF16)

        def project(bank, g, y, w_codes, columns):
            tokens = slice(P * y, P * (y + 1))
            nc.tensor.matmul_mx(
                out=bank,
                lhsT=x_codes[:, g, tokens].bitcast(FP8X4),
                lhsT_scale=x_planes[:, g, tokens],
                rhs=w_codes.bitcast(FP8X4),
                rhs_scale=w_plane(g, columns),
                start=(g == 0),
                stop=(g == GROUPS - 1),
            )

        early_banks = []
        with tc.tile_pool(name="stream", bufs=LOADS_AHEAD) as stream, tc.tile_pool(name="turn", bufs=2) as turn:
            x_chunks = {}
            w_chunks = {}
            x_sorted = {}
            x_grouped = {}

            def load_x(s):
                x_chunk = stream.tile([P, PACK, CHUNK], BF16)
                nc.sync.dma_start(out=x_chunk[:], in_=x_rows[:, :, CHUNK * s : CHUNK * (s + 1)])
                x_chunks[s] = x_chunk

            def load_w(s):
                if (STEP_GROUPS * s) % PLANES == 0:
                    load_planes(STEP_GROUPS * s // PLANES, slice(0, EARLY))
                w_chunk = stream.tile([P, STEP_GROUPS, EARLY], I32, align_bytes=64)
                if s == 0:
                    for local in range(STEP_GROUPS):
                        nc.sync.dma_start(out=w_chunk[:, local, :], in_=w_words[:, local, 0:EARLY])
                else:
                    nc.sync.dma_start(out=w_chunk[:], in_=w_words[:, STEP_GROUPS * s : STEP_GROUPS * (s + 1), 0:EARLY])
                w_chunks[s] = w_chunk

            def load_step(s):
                if s + 1 < STEPS:
                    load_x(s + 1)
                load_w(s)
                if s == STEPS - 1:
                    for a in range(GROUPS // PLANES):
                        load_planes(a, slice(EARLY, DM))
                    for a in range(GROUPS // LATE_GROUPS):
                        part = slice(LATE_GROUPS * a, LATE_GROUPS * (a + 1))
                        nc.sync.dma_start(out=w_late[:, part, :], in_=w_words[:, part, EARLY:DM])

            def sort_x(s):
                words = turn.tile([P, PACK * STEP_GROUPS, 2, P], F32, tag="x_sorted")
                nc.vector.tensor_copy(
                    out=words[:],
                    in_=x_chunks[s][:].bitcast(F32).rearrange("x y (l r w) -> x (y l) w r", l=STEP_GROUPS, w=2),
                )
                x_sorted[s] = words

            def transpose_x(s):
                for local in range(STEP_GROUPS):
                    grouped = turn.tile([P, N * PACK], BF16, tag="x_grouped", align_bytes=64)
                    x_grouped[STEP_GROUPS * s + local] = grouped
                    for half in range(2):
                        bank = psum.tile([P, 2, 2, P], F32, tag="work")
                        for y in range(2):
                            for w in range(2):
                                nc.tensor.transpose(
                                    bank[:, w, y, :],
                                    x_sorted[s][:, STEP_GROUPS * (2 * half + y) + local, w, :],
                                    ident_f32[:],
                                )
                        nc.scalar.copy(
                            out=grouped[:]
                            .bitcast(F32)[:, N * half : N * (half + 1)]
                            .rearrange("r (c w) -> r c w", w=2),
                            in_=bank[:].rearrange("r w y x -> r (y x) w"),
                        )

            def quantise_x(s):
                for g in range(STEP_GROUPS * s, STEP_GROUPS * (s + 1)):
                    nc.vector.quantize_mx(
                        out=x_codes[:, g, :].bitcast(FP8X4), scales=x_planes[:, g, :], in_=x_grouped[g][:]
                    )

            load_qk(0)
            load_x(0)
            load_qk(1)
            for s in range(LOADS_AHEAD - 1):
                load_step(s)

            def transpose_qk(h):
                q_bank = psum.tile([P, PACK, P], BF16, tag="acc")
                k_bank = psum.tile([P, PACK, P], BF16, tag="work")
                for y in range(PACK):
                    nc.tensor.transpose(q_bank[:, y, :], q_rows[:, h, y, :], ident_bf[:])
                for y in range(PACK):
                    nc.tensor.transpose(k_bank[:, y, :], k_rows[:, h, y, :], ident_bf[:])
                nc.vector.tensor_copy(out=q_t[:, h], in_=q_bank[:])
                nc.scalar.copy(
                    out=k_t[:, h].rearrange("d (w z e) -> d w z e", w=2, e=2),
                    in_=k_bank[:].rearrange("d (w e) z -> d w z e", e=2),
                )

            def score_bank(h, u, tag):
                bank = psum.tile([P, N], F32, tag=tag)
                nc.tensor.matmul(
                    bank[:], lhsT=q_t[:, h, u, :], rhs=k_t[:, h], start=True, stop=True
                )
                return bank

            def score_tiles(h):
                for u in range(PACK):
                    bank = score_bank(h, u, "acc")
                    nc.vector.tensor_tensor(
                        out=by_pair(scores[:, PACK * h + u, :]), in0=by_pair(bank[:]), in1=band_of(u), op=ALU.min
                    )
                    bank = score_bank(h + 2, u, "work")
                    if PACK * (h + 2) + u in MASKED_AT_ONCE:
                        nc.vector.tensor_tensor(
                            out=by_pair(scores[:, PACK * (h + 2) + u, :]), in0=by_pair(bank[:]), in1=band_of(u), op=ALU.min
                        )
                    else:
                        nc.scalar.copy(out=scores[:, PACK * (h + 2) + u, :], in_=bank[:])

            transpose_qk(0)
            transpose_qk(2)
            sort_x(0)
            load_step(LOADS_AHEAD - 1)
            score_tiles(0)
            transpose_qk(1)
            transpose_qk(3)
            sort_x(1)
            transpose_x(0)
            score_tiles(1)
            quantise_x(0)

            for y in range(PACK):
                early_banks.append(psum.tile([P, EARLY], F32, tag="acc", name="early%d" % y))
            for s in range(STEPS):
                row_maxima(s, 1)
                if s + SORT_AHEAD < STEPS:
                    sort_x(s + SORT_AHEAD)
                if s + 1 < STEPS:
                    transpose_x(s + 1)
                for local in range(STEP_GROUPS):
                    for y in range(PACK):
                        project(
                            early_banks[y][:], STEP_GROUPS * s + local, y, w_chunks[s][:, local, :], slice(0, EARLY)
                        )
                if s + LOADS_AHEAD < STEPS:
                    load_step(s + LOADS_AHEAD)
                exponentials(s, 1)
                if s + 1 < STEPS:
                    quantise_x(s + 1)

        with tc.tile_pool(name="late", bufs=1) as late:
            v_rounded = late.tile([P, H, PACK, DV], BF16)
            v_grouped = late.tile([P, H, DV, PACK], BF16, align_bytes=64)
            e_grouped = late.tile([P, H, PACK, P, PACK], BF16, align_bytes=64)
            e_banks = {}
            result = late.tile([P, H, PACK, DV], F32)

            def round_values(h, y, product):
                nc.scalar.copy(out=v_rounded[:, h, y, :], in_=product)

            def regroup_values(h):
                nc.vector.tensor_copy(out=v_grouped[:, h], in_=v_rounded[:, h].rearrange("x y c -> x c y"))

            def quantise_values(h):
                nc.vector.quantize_mx(
                    out=v_codes[:, h, :].bitcast(FP8X4),
                    scales=v_planes[:, h, :],
                    in_=v_grouped[:, h].rearrange("x c y -> x (c y)"),
                )

            def transpose_weights(h):
                for half in range(2):
                    bank = psum.tile([P, 2, 2, P], F32, tag="work")
                    e_banks[(h, half)] = bank
                    for u in range(2):
                        words = weights[:, PACK * h + 2 * half + u, :].bitcast(F32)
                        for w in range(2):
                            nc.tensor.transpose(bank[:, u, w, :], words[:, P * w : P * (w + 1)], ident_f32[:])

            def regroup_weights(h, half):
                target = (
                    e_grouped[:, h, 2 * half : 2 * half + 2, :, :]
                    .rearrange("z u x y -> z (u x y)")
                    .bitcast(F32)
                    .rearrange("z (u x w) -> z u x w", u=2, w=2)
                )
                source = e_banks[(h, half)][:].rearrange("z u w x -> z u x w")
                if half == 0:
                    nc.scalar.copy(out=target, in_=source)
                else:
                    nc.vector.tensor_copy(out=target, in_=source)

            def quantise_weights(h):
                nc.vector.quantize_mx(
                    out=e_codes[:, h, :].bitcast(FP8X4),
                    scales=e_planes[:, h, :],
                    in_=e_grouped[:, h].rearrange("z u x y -> z (u x y)"),
                )

            def attend(h):
                rows = out[0, h].rearrange("(x u) c -> x u c", u=PACK)
                for half in range(2):
                    bank = psum.tile([P, 2, DV], F32, tag="work")
                    for local in range(2):
                        queries = slice(P * (2 * half + local), P * (2 * half + local + 1))
                        nc.tensor.matmul_mx(
                            out=bank[:, local, :],
                            lhsT=e_codes[:, h, queries].bitcast(FP8X4),
                            lhsT_scale=e_planes[:, h, queries],
                            rhs=v_codes[:, h, :].bitcast(FP8X4),
                            rhs_scale=v_planes[:, h, :],
                            start=True,
                            stop=True,
                        )
                    for local in range(2):
                        u = 2 * half + local
                        nc.scalar.activation(
                            out=result[:, h, u, :],
                            in_=bank[:, local, :],
                            func=FUNC.Silu,
                            scale=inv_den[:, PACK * h + u : PACK * h + u + 1],
                        )
                    done = slice(2 * half, 2 * half + 2)
                    nc.sync.dma_start(out=rows[:, done, :], in_=result[:, h, done, :])

            def project_late(bank, h, y, g):
                project(bank, g, y, w_late[:, g, DV * h - EARLY : DV * (h + 1) - EARLY], slice(DV * h, DV * (h + 1)))

            def last_head(y):
                bank = psum.tile([P, DV], F32, tag="acc")
                for g in range(GROUPS):
                    project_late(bank[:], H - 1, y, g)
                round_values(H - 1, y, bank[:])

            HALF = DV // 2

            def last_product_half(part):
                h = H - 1
                y = PACK - 1
                bank = psum.tile([P, HALF], F32, tag="acc")
                first = DV * h + HALF * part
                for g in range(GROUPS):
                    project(bank[:], g, y, w_late[:, g, first - EARLY : first - EARLY + HALF], slice(first, first + HALF))
                nc.vector.tensor_copy(out=v_grouped[:, h, HALF * part : HALF * (part + 1), y], in_=bank[:])

            def regroup_first_three():
                h = H - 1
                nc.vector.tensor_copy(
                    out=v_grouped[:, h, :, 0 : PACK - 1], in_=v_rounded[:, h, 0 : PACK - 1, :].rearrange("x y c -> x c y")
                )

            def finish_values_half(part):
                h = H - 1
                columns = slice(HALF * part, HALF * (part + 1))
                nc.vector.quantize_mx(
                    out=v_codes[:, h, columns].bitcast(FP8X4),
                    scales=v_planes[:, h, columns],
                    in_=v_grouped[:, h, columns, :].rearrange("x c y -> x (c y)"),
                )

            def attend_half(part):
                h = H - 1
                columns = slice(HALF * part, HALF * (part + 1))
                banks = []
                for u in range(PACK):
                    banks.append(psum.tile([P, HALF], F32, tag="work", name="last%d" % u))
                    queries = slice(P * u, P * (u + 1))
                    nc.tensor.matmul_mx(
                        out=banks[u][:],
                        lhsT=e_codes[:, h, queries].bitcast(FP8X4),
                        lhsT_scale=e_planes[:, h, queries],
                        rhs=v_codes[:, h, columns].bitcast(FP8X4),
                        rhs_scale=v_planes[:, h, columns],
                        start=True,
                        stop=True,
                    )
                rows = out[0, h].rearrange("(x u) c -> x u c", u=PACK)
                for u in range(PACK):
                    nc.scalar.activation(
                        out=result[:, h, u, columns],
                        in_=banks[u][:],
                        func=FUNC.Silu,
                        scale=inv_den[:, PACK * h + u : PACK * h + u + 1],
                    )
                    if part == 1:
                        nc.sync.dma_start(out=rows[:, u, columns], in_=result[:, h, u, columns])
                if part == 0:
                    nc.sync.dma_start(out=rows[:, :, columns], in_=result[:, h, :, columns])

            for y in range(PACK):
                for h in range(2):
                    round_values(h, y, early_banks[y][:, DV * h : DV * (h + 1)])
            transpose_weights(0)
            transpose_weights(1)
            regroup_weights(0, 0)
            regroup_weights(1, 0)
            banks_2 = []
            for y in range(PACK):
                banks_2.append(psum.tile([P, DV], F32, tag="acc", name="head2_%d" % y))
            for a in range(GROUPS // LATE_GROUPS):
                first = TILES // 2 + 2 * a
                mask_in_sbuf(first)
                mask_in_sbuf(first + 1)
                row_maxima(first, 2)
                exponentials(first, 2)
                for y in range(PACK):
                    for g in range(LATE_GROUPS * a, LATE_GROUPS * (a + 1)):
                        project_late(banks_2[y][:], 2, y, g)
            for y in range(PACK):
                round_values(2, y, banks_2[y][:])
            regroup_weights(0, 1)
            regroup_weights(1, 1)
            regroup_values(0)
            regroup_values(1)
            quantise_weights(0)
            quantise_weights(1)
            quantise_values(0)
            quantise_values(1)
            transpose_weights(2)
            transpose_weights(3)
            regroup_weights(2, 0)
            regroup_weights(3, 0)
            regroup_weights(2, 1)
            regroup_weights(3, 1)
            last_head(0)
            denominators()
            attend(0)
            attend(1)
            regroup_values(2)
            quantise_weights(2)
            quantise_weights(3)
            quantise_values(2)
            last_head(1)
            last_head(2)
            regroup_first_three()
            last_product_half(0)
            finish_values_half(0)
            attend(2)
            last_product_half(1)
            finish_values_half(1)
            attend_half(0)
            attend_half(1)
